import numpy as np
import ml_dtypes


def mxq(x, axis, fmt="e4m3"):
    dtype, down = {"e4m3": (ml_dtypes.float8_e4m3fn, 7), "e5m2": (ml_dtypes.float8_e5m2, 14)}[fmt]
    v = np.moveaxis(np.asarray(x, np.float32).astype(ml_dtypes.bfloat16).astype(np.float64), axis, -1)
    blocks = v.reshape(v.shape[:-1] + (-1, 32))
    amax = np.abs(blocks).max(-1, keepdims=True)
    byte = np.maximum(np.where(amax > 0, np.frexp(amax)[1] - 1 + 127, 0) - down, 1)
    scale = np.exp2(byte - 127.0)
    codes = (blocks / scale).astype(np.float32).astype(dtype).astype(np.float64)
    return np.moveaxis((codes * scale).reshape(v.shape), -1, axis)


WIDE = False


def mx_kscale(k):
    if not WIDE:
        return np.ones(k)
    levels = np.array([10, -10, 5, -5, 0])
    a = np.random.permutation(np.resize(levels, k // 512 * 4)).reshape(k // 512, 4)
    idx = np.arange(k)
    return np.exp2(a[idx // 512, idx % 128 // 32])


BF16 = ml_dtypes.bfloat16


def bf(x):
    return np.asarray(x, np.float32).astype(BF16)


def f64(x):
    return np.asarray(x).astype(np.float64)


B, S, D, H, DC, DR = 4, 1024, 512, 16, 512, 64
HALF = DR // 2
ROPE_BASE = 10000.0


def rope_tables():
    inv_freq = 1.0 / ROPE_BASE ** (np.arange(0, DR, 2) / DR)
    ang = np.arange(S)[:, None] * inv_freq[None, :]
    return np.cos(ang), np.sin(ang)


def setup_inputs():
    s = mx_kscale(D)
    t = np.array(mx_kscale(DC), dtype=np.float64)
    t[HALF:DR] = t[:HALF]
    return {"x": bf(np.random.standard_normal((B, S, D)) * s),
            "W_c": bf(np.random.standard_normal((D, DC)) / np.sqrt(D) / s[:, None] * t),
            "b_c": bf(np.random.standard_normal(DC) * 0.3 * t),
            "W_d": bf(np.random.standard_normal((DC, 3 * D)) / np.sqrt(DC) / t[:, None]),
            "b_d": bf(np.random.standard_normal(3 * D) * 0.3)}


def reference(x, W_c, b_c, W_d, b_d):
    cos, sin = rope_tables()
    c = (mxq(f64(x), 2, "e4m3") @ mxq(f64(W_c), 0, "e4m3")) + f64(b_c)
    c1, c2 = c[..., :HALF], c[..., HALF:DR]
    c = np.concatenate([c1 * cos - c2 * sin, c1 * sin + c2 * cos, c[..., DR:]], axis=-1)
    return (mxq(c, 2, "e4m3") @ mxq(f64(W_d), 0, "e4m3")) + f64(b_d)

@@ -1,0 +1,296 @@
+import math
+from contextlib import ExitStack
+
+import concourse.mybir as mybir
+from concourse.masks import make_identity
+
+F32 = mybir.dt.float32
+BF16 = mybir.dt.bfloat16
+I32 = mybir.dt.int32
+U32 = mybir.dt.uint32
+U8 = mybir.dt.uint8
+FP8X4 = mybir.dt.float8_e4m3fn_x4
+ADD = mybir.AluOpType.add
+SUBTRACT = mybir.AluOpType.subtract
+MULT = mybir.AluOpType.mult
+SIN = mybir.ActivationFunctionType.Sin
+
+B, S, D, DC, DR, OUT = 4, 1024, 512, 512, 64, 1536
+HALF = DR // 2
+ROPE_BASE = 10000.0
+
+P = 128
+PACK = 4
+TILES = 4
+GROUP = TILES * P
+GROUPS = B * S // GROUP
+GROUPS_PER_SEQUENCE = S // GROUP
+BANK = 512
+OUT_BANKS = OUT // BANK
+ROT_P = DR // PACK
+PAIRED = 2 * DR
+ROUND_MAGIC = 1.5 * 2.0**23
+LAG_C, LAG_R, LAG_OUT = 1, 2, 3
+RESULT_BUFS = 2 * TILES
+TWO_BANK_TILES = 2
+
+FLOPS = 2 * B * S * D * DC + 2 * B * S * DC * OUT
+
+
+def append_partners(engine, cols):
+    slots = cols[:, 0:DC, :].rearrange("q (t p) w -> q t p w", t=PACK)
+    paired = cols[:, DC : DC + PAIRED, :].rearrange("q (s t p) w -> q s t p w", s=2, t=PACK)
+    far = ROT_P // 2
+    engine.tensor_copy(out=paired[:, 0], in_=slots[:, :, 0:ROT_P, :])
+    engine.tensor_copy(out=paired[:, 1, :, 0:far, :], in_=slots[:, :, far:ROT_P, :])
+    engine.tensor_copy(out=paired[:, 1, :, far:ROT_P, :], in_=slots[:, :, 0:far, :])
+
+
+def tile_deepseekmla_pa_t_kernel(tc, x, W_c, b_c, W_d, b_d, out):
+    nc = tc.nc
+    x_groups = x.flatten_outer_dims().rearrange("(g p a) d -> g p (a d)", p=P, a=TILES)
+    out_groups = out.flatten_outer_dims().rearrange("(g p a) c -> g p a c", p=P, a=TILES)
+
+    with ExitStack() as ctx:
+        consts = ctx.enter_context(tc.tile_pool(name="consts", bufs=1))
+        work = ctx.enter_context(tc.tile_pool(name="work", bufs=3))
+        results = ctx.enter_context(tc.tile_pool(name="results", bufs=RESULT_BUFS))
+        front_psum = ctx.enter_context(tc.psum_pool(name="front_psum", bufs=4))
+        out_psum = ctx.enter_context(tc.psum_pool(name="out_psum", bufs=4))
+        ctx.enter_context(tc.manual_schedule())
+
+        wc_raw = consts.tile([P, PACK, DC], BF16)
+        nc.sync.dma_start(
+            out=wc_raw[:].rearrange("q (u e) c -> q u (e c)", u=2),
+            in_=W_c.rearrange("(u q e) c -> q u (e c)", u=2, e=2),
+        )
+        x_sb = []
+        for g in range(GROUPS):
+            x_sb.append(consts.tile([P, TILES * D], BF16, name="x_sb%d" % g))
+        bc_raw = consts.tile([P, DC], BF16)
+        nc.sync.dma_start(out=bc_raw[:], in_=b_c.partition_broadcast(P))
+        for g in range(2):
+            nc.sync.dma_start(out=x_sb[g][:], in_=x_groups[g])
+        wd_raw = consts.tile([P, PACK, OUT], BF16)
+        wd_rows = W_d.rearrange("(p t) c -> p t c", t=PACK)
+        for n in range(OUT_BANKS):
+            nc.sync.dma_start(
+                out=wd_raw[:, :, n * BANK : (n + 1) * BANK],
+                in_=wd_rows[:, :, n * BANK : (n + 1) * BANK],
+            )
+        bd_all = consts.tile([P, OUT], BF16)
+        nc.sync.dma_start(out=bd_all[:], in_=b_d.partition_broadcast(P))
+        for g in range(2, GROUPS):
+            nc.sync.dma_start(out=x_sb[g][:], in_=x_groups[g])
+
+        position = consts.tile([P, GROUPS_PER_SEQUENCE * TILES, 1], I32)
+        nc.gpsimd.iota(
+            position[:], pattern=[[GROUP, GROUPS_PER_SEQUENCE], [1, TILES]], base=0, channel_multiplier=TILES
+        )
+        ident_f32 = consts.tile([P, P], F32)
+        make_identity(nc, ident_f32[:])
+        ident_bf16 = consts.tile([P, P], BF16)
+        make_identity(nc, ident_bf16[:])
+        turns = consts.tile([P, 2, GROUPS_PER_SEQUENCE * TILES, HALF], F32)
+        for j in range(HALF):
+            column = (j % PACK) * (HALF // PACK) + j // PACK
+            nc.vector.tensor_scalar_mul(
+                out=turns[:, 0, :, column : column + 1],
+                in0=position[:],
+                scalar1=1.0 / ROPE_BASE ** (2.0 * j / DR) / (2.0 * math.pi),
+            )
+
+        wc_grouped = consts.tile([P, DC + PAIRED, PACK], BF16, align_bytes=64)
+        nc.vector.tensor_copy(
+            out=wc_grouped[:, 0:DC, :].rearrange("q (t p) k -> q t p k", t=PACK),
+            in_=wc_raw[:].rearrange("q k (p t) -> q t p k", t=PACK),
+        )
+        append_partners(nc.vector, wc_grouped[:])
+        wc_codes = consts.tile([P, DC + PAIRED], U32, align_bytes=64)
+        wc_scales = consts.tile([P, DC + PAIRED], U8, align_bytes=64)
+        for cols in (slice(0, DC), slice(DC, DC + PAIRED)):
+            nc.vector.quantize_mx(
+                out=wc_codes[:, cols].bitcast(FP8X4),
+                scales=wc_scales[:, cols],
+                in_=wc_grouped[:, cols, :].rearrange("q c k -> q (c k)"),
+            )
+        bc_cols = consts.tile([P, DC + PAIRED, 1], F32)
+        nc.gpsimd.tensor_copy(
+            out=bc_cols[:, 0:DC, 0].rearrange("q (t p) -> q t p", t=PACK),
+            in_=bc_raw[:].rearrange("q (p t) -> q t p", t=PACK),
+        )
+        append_partners(nc.gpsimd, bc_cols[:])
+
+        nc.vector.tensor_scalar_add(out=turns[:, 1], in0=turns[:, 0], scalar1=0.25)
+        whole = consts.tile([P, 2, GROUPS_PER_SEQUENCE * TILES, HALF], F32)
+        nc.vector.tensor_scalar(
+            out=whole[:], in0=turns[:], scalar1=ROUND_MAGIC, scalar2=ROUND_MAGIC, op0=ADD, op1=SUBTRACT
+        )
+        nc.vector.tensor_tensor(out=turns[:], in0=turns[:], in1=whole[:], op=SUBTRACT)
+        table = consts.tile([P, GROUPS_PER_SEQUENCE * TILES, PAIRED], F32)
+        table_parts = table[:].rearrange("p g (s t h i) -> p g s t h i", s=2, t=PACK, h=2)
+        sin_turns = turns[:, 0].rearrange("p g (t i) -> p g t i", t=PACK)
+        cos_turns = turns[:, 1].rearrange("p g (t i) -> p g t i", t=PACK)
+
+        def fill_table():
+            nc.scalar.activation(out=table_parts[:, :, 0, :, 0, :], in_=cos_turns, func=SIN, scale=2.0 * math.pi)
+            nc.scalar.activation(out=table_parts[:, :, 0, :, 1, :], in_=cos_turns, func=SIN, scale=2.0 * math.pi)
+            nc.scalar.activation(out=table_parts[:, :, 1, :, 0, :], in_=sin_turns, func=SIN, scale=-2.0 * math.pi)
+            nc.scalar.activation(out=table_parts[:, :, 1, :, 1, :], in_=sin_turns, func=SIN, scale=2.0 * math.pi)
+
+        wd_grouped = consts.tile([P, OUT, PACK], BF16, align_bytes=64)
+        wd_codes = consts.tile([P, OUT], U32, align_bytes=64)
+        wd_scales = consts.tile([P, OUT], U8, align_bytes=64)
+
+        def regroup_wd():
+            views = []
+            for n in range(OUT_BANKS):
+                cols = slice(n * BANK, (n + 1) * BANK)
+                views.append(
+                    (
+                        wd_grouped[:, cols, :].rearrange("p (c i) t -> p c t i", i=4),
+                        wd_raw[:, :, cols].rearrange("p t (c i) -> p c t i", i=4),
+                    )
+                )
+            nc.scalar.copy(out=views[0][0], in_=views[0][1])
+            nc.vector.tensor_copy(out=views[1][0], in_=views[1][1])
+            nc.gpsimd.tensor_scalar(out=views[2][0], in0=views[2][1], scalar1=1.0, scalar2=0.0, op0=MULT, op1=ADD)
+
+        def quantise_wd():
+            for n in range(OUT_BANKS):
+                cols = slice(n * BANK, (n + 1) * BANK)
+                nc.vector.quantize_mx(
+                    out=wd_codes[:, cols].bitcast(FP8X4),
+                    scales=wd_scales[:, cols],
+                    in_=wd_grouped[:, cols, :].rearrange("p c t -> p (c t)"),
+                )
+
+        grouped_x, x_codes, x_scales, r_rows, products, grouped_r, r_codes, r_scales = {}, {}, {}, {}, {}, {}, {}, {}
+
+        def transpose_x(g, a):
+            if a == 0:
+                grouped_x[g] = work.tile([P, GROUP * PACK], BF16, align_bytes=64, name="grouped_x")
+            x_words = x_sb[g][:].bitcast(F32)
+            grouped_words = grouped_x[g][:].bitcast(F32).rearrange("q (a n u) -> q a n u", a=TILES, u=2)
+            xt = front_psum.tile([P, 2, P], F32, tag="front")
+            for u in range(2):
+                first = (a * 2 + u) * P
+                nc.tensor.transpose(xt[:, u, :], x_words[:, first : first + P], ident_f32[:])
+            nc.scalar.copy(out=grouped_words[:, a], in_=xt[:].rearrange("q u n -> q n u"))
+
+        def quantise_x(g):
+            x_codes[g] = work.tile([P, GROUP], U32, align_bytes=64, name="x_codes")
+            x_scales[g] = work.tile([P, GROUP], U8, align_bytes=64, name="x_scales")
+            nc.vector.quantize_mx(out=x_codes[g][:].bitcast(FP8X4), scales=x_scales[g][:], in_=grouped_x[g][:])
+
+        def first_product(acc, g, a, cols):
+            tokens = slice(a * P, (a + 1) * P)
+            nc.tensor.matmul_mx(
+                out=acc,
+                lhsT=x_codes[g][:, tokens].bitcast(FP8X4),
+                lhsT_scale=x_scales[g][:, tokens],
+                rhs=wc_codes[:, cols].bitcast(FP8X4),
+                rhs_scale=wc_scales[:, cols],
+                start=True,
+                stop=True,
+            )
+
+        def paired_columns(g):
+            r_rows[g] = work.tile([P, TILES, PACK, P], BF16, name="r_rows")
+            paired = front_psum.tile([P, TILES, PAIRED], F32, tag="front")
+            for a in range(TILES):
+                first_product(paired[:, a, :], g, a, slice(DC, DC + PAIRED))
+            products[g] = work.tile([P, TILES, PAIRED], F32, name="products")
+            nc.vector.tensor_tensor(
+                out=products[g][:],
+                in0=paired[:],
+                in1=bc_cols[:, DC : DC + PAIRED, 0].unsqueeze(1).to_broadcast([P, TILES, PAIRED]),
+                op=ADD,
+            )
+
+        def rotate(g, engine):
+            h = g % GROUPS_PER_SEQUENCE
+            engine.tensor_tensor(
+                out=products[g][:], in0=products[g][:], in1=table[:, h * TILES : (h + 1) * TILES, :], op=MULT
+            )
+            engine.tensor_tensor(
+                out=r_rows[g][:, :, :, 0:ROT_P],
+                in0=products[g][:, :, 0:DR].rearrange("n a (t p) -> n a t p", t=PACK),
+                in1=products[g][:, :, DR:PAIRED].rearrange("n a (t p) -> n a t p", t=PACK),
+                op=ADD,
+            )
+
+        def other_columns(g, a):
+            c_acc = front_psum.tile([P, PACK, P], F32, tag="front")
+            first_product(c_acc[:].rearrange("n t p -> n (t p)"), g, a, slice(0, DC))
+            nc.vector.tensor_tensor(
+                out=r_rows[g][:, a, :, ROT_P:P],
+                in0=c_acc[:, :, ROT_P:P],
+                in1=bc_cols[:, 0:DC, 0].rearrange("n (t p) -> n t p", t=PACK)[:, :, ROT_P:P],
+                op=ADD,
+            )
+
+        def transpose_r(g, a):
+            if a == 0:
+                grouped_r[g] = work.tile([P, TILES, P, PACK], BF16, align_bytes=64, name="grouped_r")
+            rt = front_psum.tile([P, PACK, P], BF16, tag="front")
+            for t in range(PACK):
+                nc.tensor.transpose(rt[:, t, :], r_rows[g][:, a, t, :], ident_bf16[:])
+            nc.scalar.copy(out=grouped_r[g][:, a], in_=rt[:].rearrange("p t n -> p n t"))
+
+        def quantise_r(g):
+            r_codes[g] = work.tile([P, GROUP], U32, align_bytes=64, name="r_codes")
+            r_scales[g] = work.tile([P, GROUP], U8, align_bytes=64, name="r_scales")
+            nc.vector.quantize_mx(
+                out=r_codes[g][:].bitcast(FP8X4),
+                scales=r_scales[g][:],
+                in_=grouped_r[g][:].rearrange("p a n t -> p (a n t)"),
+            )
+
+        def second_product(g, a):
+            tokens = slice(a * P, (a + 1) * P)
+            result = results.tile([P, OUT], F32)
+            for n in range(OUT_BANKS):
+                cols = slice(n * BANK, (n + 1) * BANK)
+                acc = out_psum.tile([P, BANK], F32)
+                nc.tensor.matmul_mx(
+                    out=acc[:],
+                    lhsT=r_codes[g][:, tokens].bitcast(FP8X4),
+                    lhsT_scale=r_scales[g][:, tokens],
+                    rhs=wd_codes[:, cols].bitcast(FP8X4),
+                    rhs_scale=wd_scales[:, cols],
+                    start=True,
+                    stop=True,
+                )
+                if n == 0 or (n == 2 and (a < TWO_BANK_TILES or g + LAG_OUT - LAG_C >= GROUPS)):
+                    nc.vector.tensor_tensor(out=result[:, cols], in0=acc[:], in1=bd_all[:, cols], op=ADD)
+                else:
+                    nc.scalar.copy(out=result[:, cols], in_=acc[:])
+                    nc.gpsimd.tensor_tensor(out=result[:, cols], in0=result[:, cols], in1=bd_all[:, cols], op=ADD)
+            nc.sync.dma_start(out=out_groups[g][:, a, :], in_=result[:])
+
+        for step in range(GROUPS + LAG_OUT):
+            g_x, g_c, g_r, g_out = step, step - LAG_C, step - LAG_R, step - LAG_OUT
+            for a in range(TILES):
+                if 0 <= g_r < GROUPS:
+                    transpose_r(g_r, a)
+                if g_x < GROUPS:
+                    transpose_x(g_x, a)
+                if 0 <= g_c < GROUPS:
+                    if a == 0:
+                        paired_columns(g_c)
+                    other_columns(g_c, a)
+                if 0 <= g_out:
+                    second_product(g_out, a)
+            if step == 0:
+                fill_table()
+            if g_x < GROUPS:
+                quantise_x(g_x)
+            if step == LAG_C:
+                regroup_wd()
+            if 0 <= g_c < GROUPS:
+                rotate(g_c, nc.vector if 0 <= g_out else nc.gpsimd)
+            if step == LAG_C:
+                quantise_wd()
+            if 0 <= g_r < GROUPS:
+                quantise_r(g_r)

@@ -32,7 +32,7 @@ PAIRED = 2 * DR
 ROUND_MAGIC = 1.5 * 2.0**23
 LAG_C, LAG_R, LAG_OUT = 1, 2, 3
 RESULT_BUFS = 2 * TILES
-TWO_BANK_TILES = 2
+TWO_BANK_TILES = 4
 
 FLOPS = 2 * B * S * D * DC + 2 * B * S * DC * OUT
 

@@ -32,7 +32,8 @@ PAIRED = 2 * DR
 ROUND_MAGIC = 1.5 * 2.0**23
 LAG_C, LAG_R, LAG_OUT = 1, 2, 3
 RESULT_BUFS = 2 * TILES
-TWO_BANK_TILES = 4
+VECTOR_TAKES_ALL = True
+TWO_BANK_TILES = 2
 
 FLOPS = 2 * B * S * D * DC + 2 * B * S * DC * OUT
 
@@ -262,7 +263,7 @@ def tile_deepseekmla_pa_t_kernel(tc, x, W_c, b_c, W_d, b_d, out):
                     start=True,
                     stop=True,
                 )
-                if n == 0 or (n == 2 and (a < TWO_BANK_TILES or g + LAG_OUT - LAG_C >= GROUPS)):
+                if VECTOR_TAKES_ALL or n == 0 or (n == 2 and (a < TWO_BANK_TILES or g + LAG_OUT - LAG_C >= GROUPS)):
                     nc.vector.tensor_tensor(out=result[:, cols], in0=acc[:], in1=bd_all[:, cols], op=ADD)
                 else:
                     nc.scalar.copy(out=result[:, cols], in_=acc[:])

import math
from contextlib import ExitStack

import concourse.mybir as mybir
from concourse.masks import make_identity

F32 = mybir.dt.float32
BF16 = mybir.dt.bfloat16
I32 = mybir.dt.int32
U32 = mybir.dt.uint32
U8 = mybir.dt.uint8
FP8X4 = mybir.dt.float8_e4m3fn_x4
ADD = mybir.AluOpType.add
SUBTRACT = mybir.AluOpType.subtract
MULT = mybir.AluOpType.mult
SIN = mybir.ActivationFunctionType.Sin

B, S, D, DC, DR, OUT = 4, 1024, 512, 512, 64, 1536
HALF = DR // 2
ROPE_BASE = 10000.0

P = 128
PACK = 4
TILES = 4
GROUP = TILES * P
GROUPS = B * S // GROUP
GROUPS_PER_SEQUENCE = S // GROUP
BANK = 512
OUT_BANKS = OUT // BANK
ROT_P = DR // PACK
PAIRED = 2 * DR
ROUND_MAGIC = 1.5 * 2.0**23
LAG_C, LAG_R, LAG_OUT = 1, 2, 3
RESULT_BUFS = 2 * TILES
VECTOR_TAKES_ALL = True
TWO_BANK_TILES = 2

FLOPS = 2 * B * S * D * DC + 2 * B * S * DC * OUT


def append_partners(engine, cols):
    slots = cols[:, 0:DC, :].rearrange("q (t p) w -> q t p w", t=PACK)
    paired = cols[:, DC : DC + PAIRED, :].rearrange("q (s t p) w -> q s t p w", s=2, t=PACK)
    far = ROT_P // 2
    engine.tensor_copy(out=paired[:, 0], in_=slots[:, :, 0:ROT_P, :])
    engine.tensor_copy(out=paired[:, 1, :, 0:far, :], in_=slots[:, :, far:ROT_P, :])
    engine.tensor_copy(out=paired[:, 1, :, far:ROT_P, :], in_=slots[:, :, 0:far, :])


def tile_deepseekmla_pa_t_kernel(tc, x, W_c, b_c, W_d, b_d, out):
    nc = tc.nc
    x_groups = x.flatten_outer_dims().rearrange("(g p a) d -> g p (a d)", p=P, a=TILES)
    out_groups = out.flatten_outer_dims().rearrange("(g p a) c -> g p a c", p=P, a=TILES)

    with ExitStack() as ctx:
        consts = ctx.enter_context(tc.tile_pool(name="consts", bufs=1))
        work = ctx.enter_context(tc.tile_pool(name="work", bufs=3))
        results = ctx.enter_context(tc.tile_pool(name="results", bufs=RESULT_BUFS))
        front_psum = ctx.enter_context(tc.psum_pool(name="front_psum", bufs=4))
        out_psum = ctx.enter_context(tc.psum_pool(name="out_psum", bufs=4))
        ctx.enter_context(tc.manual_schedule())

        wc_raw = consts.tile([P, PACK, DC], BF16)
        nc.sync.dma_start(
            out=wc_raw[:].rearrange("q (u e) c -> q u (e c)", u=2),
            in_=W_c.rearrange("(u q e) c -> q u (e c)", u=2, e=2),
        )
        x_sb = []
        for g in range(GROUPS):
            x_sb.append(consts.tile([P, TILES * D], BF16, name="x_sb%d" % g))
        bc_raw = consts.tile([P, DC], BF16)
        nc.sync.dma_start(out=bc_raw[:], in_=b_c.partition_broadcast(P))
        for g in range(2):
            nc.sync.dma_start(out=x_sb[g][:], in_=x_groups[g])
        wd_raw = consts.tile([P, PACK, OUT], BF16)
        wd_rows = W_d.rearrange("(p t) c -> p t c", t=PACK)
        for n in range(OUT_BANKS):
            nc.sync.dma_start(
                out=wd_raw[:, :, n * BANK : (n + 1) * BANK],
                in_=wd_rows[:, :, n * BANK : (n + 1) * BANK],
            )
        bd_all = consts.tile([P, OUT], BF16)
        nc.sync.dma_start(out=bd_all[:], in_=b_d.partition_broadcast(P))
        for g in range(2, GROUPS):
            nc.sync.dma_start(out=x_sb[g][:], in_=x_groups[g])

        position = consts.tile([P, GROUPS_PER_SEQUENCE * TILES, 1], I32)
        nc.gpsimd.iota(
            position[:], pattern=[[GROUP, GROUPS_PER_SEQUENCE], [1, TILES]], base=0, channel_multiplier=TILES
        )
        ident_f32 = consts.tile([P, P], F32)
        make_identity(nc, ident_f32[:])
        ident_bf16 = consts.tile([P, P], BF16)
        make_identity(nc, ident_bf16[:])
        turns = consts.tile([P, 2, GROUPS_PER_SEQUENCE * TILES, HALF], F32)
        for j in range(HALF):
            column = (j % PACK) * (HALF // PACK) + j // PACK
            nc.vector.tensor_scalar_mul(
                out=turns[:, 0, :, column : column + 1],
                in0=position[:],
                scalar1=1.0 / ROPE_BASE ** (2.0 * j / DR) / (2.0 * math.pi),
            )

        wc_grouped = consts.tile([P, DC + PAIRED, PACK], BF16, align_bytes=64)
        nc.vector.tensor_copy(
            out=wc_grouped[:, 0:DC, :].rearrange("q (t p) k -> q t p k", t=PACK),
            in_=wc_raw[:].rearrange("q k (p t) -> q t p k", t=PACK),
        )
        append_partners(nc.vector, wc_grouped[:])
        wc_codes = consts.tile([P, DC + PAIRED], U32, align_bytes=64)
        wc_scales = consts.tile([P, DC + PAIRED], U8, align_bytes=64)
        for cols in (slice(0, DC), slice(DC, DC + PAIRED)):
            nc.vector.quantize_mx(
                out=wc_codes[:, cols].bitcast(FP8X4),
                scales=wc_scales[:, cols],
                in_=wc_grouped[:, cols, :].rearrange("q c k -> q (c k)"),
            )
        bc_cols = consts.tile([P, DC + PAIRED, 1], F32)
        nc.gpsimd.tensor_copy(
            out=bc_cols[:, 0:DC, 0].rearrange("q (t p) -> q t p", t=PACK),
            in_=bc_raw[:].rearrange("q (p t) -> q t p", t=PACK),
        )
        append_partners(nc.gpsimd, bc_cols[:])

        nc.vector.tensor_scalar_add(out=turns[:, 1], in0=turns[:, 0], scalar1=0.25)
        whole = consts.tile([P, 2, GROUPS_PER_SEQUENCE * TILES, HALF], F32)
        nc.vector.tensor_scalar(
            out=whole[:], in0=turns[:], scalar1=ROUND_MAGIC, scalar2=ROUND_MAGIC, op0=ADD, op1=SUBTRACT
        )
        nc.vector.tensor_tensor(out=turns[:], in0=turns[:], in1=whole[:], op=SUBTRACT)
        table = consts.tile([P, GROUPS_PER_SEQUENCE * TILES, PAIRED], F32)
        table_parts = table[:].rearrange("p g (s t h i) -> p g s t h i", s=2, t=PACK, h=2)
        sin_turns = turns[:, 0].rearrange("p g (t i) -> p g t i", t=PACK)
        cos_turns = turns[:, 1].rearrange("p g (t i) -> p g t i", t=PACK)

        def fill_table():
            nc.scalar.activation(out=table_parts[:, :, 0, :, 0, :], in_=cos_turns, func=SIN, scale=2.0 * math.pi)
            nc.scalar.activation(out=table_parts[:, :, 0, :, 1, :], in_=cos_turns, func=SIN, scale=2.0 * math.pi)
            nc.scalar.activation(out=table_parts[:, :, 1, :, 0, :], in_=sin_turns, func=SIN, scale=-2.0 * math.pi)
            nc.scalar.activation(out=table_parts[:, :, 1, :, 1, :], in_=sin_turns, func=SIN, scale=2.0 * math.pi)

        wd_grouped = consts.tile([P, OUT, PACK], BF16, align_bytes=64)
        wd_codes = consts.tile([P, OUT], U32, align_bytes=64)
        wd_scales = consts.tile([P, OUT], U8, align_bytes=64)

        def regroup_wd():
            views = []
            for n in range(OUT_BANKS):
                cols = slice(n * BANK, (n + 1) * BANK)
                views.append(
                    (
                        wd_grouped[:, cols, :].rearrange("p (c i) t -> p c t i", i=4),
                        wd_raw[:, :, cols].rearrange("p t (c i) -> p c t i", i=4),
                    )
                )
            nc.scalar.copy(out=views[0][0], in_=views[0][1])
            nc.vector.tensor_copy(out=views[1][0], in_=views[1][1])
            nc.gpsimd.tensor_scalar(out=views[2][0], in0=views[2][1], scalar1=1.0, scalar2=0.0, op0=MULT, op1=ADD)

        def quantise_wd():
            for n in range(OUT_BANKS):
                cols = slice(n * BANK, (n + 1) * BANK)
                nc.vector.quantize_mx(
                    out=wd_codes[:, cols].bitcast(FP8X4),
                    scales=wd_scales[:, cols],
                    in_=wd_grouped[:, cols, :].rearrange("p c t -> p (c t)"),
                )

        grouped_x, x_codes, x_scales, r_rows, products, grouped_r, r_codes, r_scales = {}, {}, {}, {}, {}, {}, {}, {}

        def transpose_x(g, a):
            if a == 0:
                grouped_x[g] = work.tile([P, GROUP * PACK], BF16, align_bytes=64, name="grouped_x")
            x_words = x_sb[g][:].bitcast(F32)
            grouped_words = grouped_x[g][:].bitcast(F32).rearrange("q (a n u) -> q a n u", a=TILES, u=2)
            xt = front_psum.tile([P, 2, P], F32, tag="front")
            for u in range(2):
                first = (a * 2 + u) * P
                nc.tensor.transpose(xt[:, u, :], x_words[:, first : first + P], ident_f32[:])
            nc.scalar.copy(out=grouped_words[:, a], in_=xt[:].rearrange("q u n -> q n u"))

        def quantise_x(g):
            x_codes[g] = work.tile([P, GROUP], U32, align_bytes=64, name="x_codes")
            x_scales[g] = work.tile([P, GROUP], U8, align_bytes=64, name="x_scales")
            nc.vector.quantize_mx(out=x_codes[g][:].bitcast(FP8X4), scales=x_scales[g][:], in_=grouped_x[g][:])

        def first_product(acc, g, a, cols):
            tokens = slice(a * P, (a + 1) * P)
            nc.tensor.matmul_mx(
                out=acc,
                lhsT=x_codes[g][:, tokens].bitcast(FP8X4),
                lhsT_scale=x_scales[g][:, tokens],
                rhs=wc_codes[:, cols].bitcast(FP8X4),
                rhs_scale=wc_scales[:, cols],
                start=True,
                stop=True,
            )

        def paired_columns(g):
            r_rows[g] = work.tile([P, TILES, PACK, P], BF16, name="r_rows")
            paired = front_psum.tile([P, TILES, PAIRED], F32, tag="front")
            for a in range(TILES):
                first_product(paired[:, a, :], g, a, slice(DC, DC + PAIRED))
            products[g] = work.tile([P, TILES, PAIRED], F32, name="products")
            nc.vector.tensor_tensor(
                out=products[g][:],
                in0=paired[:],
                in1=bc_cols[:, DC : DC + PAIRED, 0].unsqueeze(1).to_broadcast([P, TILES, PAIRED]),
                op=ADD,
            )

        def rotate(g, engine):
            h = g % GROUPS_PER_SEQUENCE
            engine.tensor_tensor(
                out=products[g][:], in0=products[g][:], in1=table[:, h * TILES : (h + 1) * TILES, :], op=MULT
            )
            engine.tensor_tensor(
                out=r_rows[g][:, :, :, 0:ROT_P],
                in0=products[g][:, :, 0:DR].rearrange("n a (t p) -> n a t p", t=PACK),
                in1=products[g][:, :, DR:PAIRED].rearrange("n a (t p) -> n a t p", t=PACK),
                op=ADD,
            )

        def other_columns(g, a):
            c_acc = front_psum.tile([P, PACK, P], F32, tag="front")
            first_product(c_acc[:].rearrange("n t p -> n (t p)"), g, a, slice(0, DC))
            nc.vector.tensor_tensor(
                out=r_rows[g][:, a, :, ROT_P:P],
                in0=c_acc[:, :, ROT_P:P],
                in1=bc_cols[:, 0:DC, 0].rearrange("n (t p) -> n t p", t=PACK)[:, :, ROT_P:P],
                op=ADD,
            )

        def transpose_r(g, a):
            if a == 0:
                grouped_r[g] = work.tile([P, TILES, P, PACK], BF16, align_bytes=64, name="grouped_r")
            rt = front_psum.tile([P, PACK, P], BF16, tag="front")
            for t in range(PACK):
                nc.tensor.transpose(rt[:, t, :], r_rows[g][:, a, t, :], ident_bf16[:])
            nc.scalar.copy(out=grouped_r[g][:, a], in_=rt[:].rearrange("p t n -> p n t"))

        def quantise_r(g):
            r_codes[g] = work.tile([P, GROUP], U32, align_bytes=64, name="r_codes")
            r_scales[g] = work.tile([P, GROUP], U8, align_bytes=64, name="r_scales")
            nc.vector.quantize_mx(
                out=r_codes[g][:].bitcast(FP8X4),
                scales=r_scales[g][:],
                in_=grouped_r[g][:].rearrange("p a n t -> p (a n t)"),
            )

        def second_product(g, a):
            tokens = slice(a * P, (a + 1) * P)
            result = results.tile([P, OUT], F32)
            for n in range(OUT_BANKS):
                cols = slice(n * BANK, (n + 1) * BANK)
                acc = out_psum.tile([P, BANK], F32)
                nc.tensor.matmul_mx(
                    out=acc[:],
                    lhsT=r_codes[g][:, tokens].bitcast(FP8X4),
                    lhsT_scale=r_scales[g][:, tokens],
                    rhs=wd_codes[:, cols].bitcast(FP8X4),
                    rhs_scale=wd_scales[:, cols],
                    start=True,
                    stop=True,
                )
                if VECTOR_TAKES_ALL or n == 0 or (n == 2 and (a < TWO_BANK_TILES or g + LAG_OUT - LAG_C >= GROUPS)):
                    nc.vector.tensor_tensor(out=result[:, cols], in0=acc[:], in1=bd_all[:, cols], op=ADD)
                else:
                    nc.scalar.copy(out=result[:, cols], in_=acc[:])
                    nc.gpsimd.tensor_tensor(out=result[:, cols], in0=result[:, cols], in1=bd_all[:, cols], op=ADD)
            nc.sync.dma_start(out=out_groups[g][:, a, :], in_=result[:])

        for step in range(GROUPS + LAG_OUT):
            g_x, g_c, g_r, g_out = step, step - LAG_C, step - LAG_R, step - LAG_OUT
            for a in range(TILES):
                if 0 <= g_r < GROUPS:
                    transpose_r(g_r, a)
                if g_x < GROUPS:
                    transpose_x(g_x, a)
                if 0 <= g_c < GROUPS:
                    if a == 0:
                        paired_columns(g_c)
                    other_columns(g_c, a)
                if 0 <= g_out:
                    second_product(g_out, a)
            if step == 0:
                fill_table()
            if g_x < GROUPS:
                quantise_x(g_x)
            if step == LAG_C:
                regroup_wd()
            if 0 <= g_c < GROUPS:
                rotate(g_c, nc.vector if 0 <= g_out else nc.gpsimd)
            if step == LAG_C:
                quantise_wd()
            if 0 <= g_r < GROUPS:
                quantise_r(g_r)
